import numpy as np
import ml_dtypes


def mxq(x, axis, fmt="e4m3"):
    dtype, down = {"e4m3": (ml_dtypes.float8_e4m3fn, 7), "e5m2": (ml_dtypes.float8_e5m2, 14)}[fmt]
    v = np.moveaxis(np.asarray(x, np.float32).astype(ml_dtypes.bfloat16).astype(np.float64), axis, -1)
    blocks = v.reshape(v.shape[:-1] + (-1, 32))
    amax = np.abs(blocks).max(-1, keepdims=True)
    byte = np.maximum(np.where(amax > 0, np.frexp(amax)[1] - 1 + 127, 0) - down, 1)
    scale = np.exp2(byte - 127.0)
    codes = (blocks / scale).astype(np.float32).astype(dtype).astype(np.float64)
    return np.moveaxis((codes * scale).reshape(v.shape), -1, axis)


WIDE = False


def mx_kscale(k):
    if not WIDE:
        return np.ones(k)
    levels = np.array([10, -10, 5, -5, 0])
    a = np.random.permutation(np.resize(levels, k // 512 * 4)).reshape(k // 512, 4)
    idx = np.arange(k)
    return np.exp2(a[idx // 512, idx % 128 // 32])


BF16 = ml_dtypes.bfloat16


def bf(x):
    return np.asarray(x, np.float32).astype(BF16)


def f64(x):
    return np.asarray(x).astype(np.float64)


E2M1 = np.array([0.0, 0.5, 1.0, 1.5, 2.0, 3.0, 4.0, 6.0, -0.0, -0.5, -1.0, -1.5, -2.0, -3.0, -4.0, -6.0])


def pack_weight(w, fmt):
    k, n = w.shape
    w = f64(bf(w)).reshape(k // 32, 32, n)
    amax = np.abs(w).max(1)
    if fmt == "e4m3":
        byte = np.frexp(amax)[1] - 1 + 127 - 7
    else:
        mant, ex = np.frexp(amax / 6.0)
        byte = np.where(mant > 0.5, ex, ex - 1) + 127
    byte = np.clip(np.where(amax > 0, byte, 1), 1, 254)
    scaled = (w * np.exp2(127.0 - byte)[:, None, :]).reshape(k, n).astype(np.float32)
    by_word = np.ascontiguousarray(scaled.reshape(k // 512, 128, 4, n).transpose(0, 1, 3, 2))
    if fmt == "e4m3":
        words = by_word.astype(ml_dtypes.float8_e4m3fn).view(np.uint8)
    else:
        c = by_word.astype(ml_dtypes.float4_e2m1fn).view(np.uint8) & 0xF
        words = c[..., 0::2] | (c[..., 1::2] << 4)
    return np.ascontiguousarray(words), np.ascontiguousarray(byte.astype(np.uint8).reshape(k // 512, 16, n))


def unpack_weight(words, scales, fmt):
    g, p, n, _ = words.shape
    if fmt == "e4m3":
        vals = np.ascontiguousarray(words).view(ml_dtypes.float8_e4m3fn).astype(np.float64)
    else:
        nib = np.empty((g, p, n, 4), np.uint8)
        nib[..., 0::2] = words & 0xF
        nib[..., 1::2] = words >> 4
        vals = E2M1[nib]
    vals = vals * np.repeat(np.exp2(scales.astype(np.float64) - 127.0), 8, axis=1)[..., None]
    return vals.transpose(0, 1, 3, 2).reshape(g * 512, n)


B, T, D, H = 8, 16, 2048, 2048
FMT = "e4m3"


def sigmoid(v):
    return 1.0 / (1.0 + np.exp(-v))


def setup_inputs():
    s = mx_kscale(D)
    x = bf(np.random.standard_normal((B, T, D)) * s)
    Wq_words, Wq_scales = pack_weight((np.random.standard_normal((H, D)) * 1.0 / np.sqrt(D) / s).T, FMT)
    bq = bf(np.random.standard_normal(H) * 0.5)
    Wk_words, Wk_scales = pack_weight((np.random.standard_normal((H, D)) * 0.6 / np.sqrt(D) / s).T, FMT)
    bk = bf(np.random.standard_normal(H) * 0.3)
    Wv_words, Wv_scales = pack_weight((np.random.standard_normal((H, D)) * 2.0 / np.sqrt(D) / s).T, FMT)
    bv = bf(np.random.standard_normal(H) * 0.5)
    wbias = bf(np.random.uniform(0.0, 1.0, H))
    return {"x": x,
            "Wq_words": Wq_words, "Wq_scales": Wq_scales,
            "bq": bq,
            "Wk_words": Wk_words, "Wk_scales": Wk_scales,
            "bk": bk,
            "Wv_words": Wv_words, "Wv_scales": Wv_scales,
            "bv": bv,
            "wbias": wbias}


def reference(x, Wq_words, Wq_scales, bq, Wk_words, Wk_scales, bk, Wv_words, Wv_scales, bv, wbias):
    xq = mxq(f64(x), 2, "e4m3")
    Q = (xq @ unpack_weight(Wq_words, Wq_scales, FMT)) + f64(bq)
    K = (xq @ unpack_weight(Wk_words, Wk_scales, FMT)) + f64(bk)
    V = (xq @ unpack_weight(Wv_words, Wv_scales, FMT)) + f64(bv)
    Q_sig = sigmoid(Q)
    numer = np.exp(K + f64(wbias))
    denom = numer.sum(axis=0)
    weighted = (numer * V).sum(axis=0) / denom
    Yt = Q_sig * weighted
    return Yt

@@ -1,0 +1,283 @@
+from contextlib import ExitStack
+
+import concourse.mybir as mybir
+from concourse.masks import make_identity
+
+FP8X4 = mybir.dt.float8_e4m3fn_x4
+F32 = mybir.dt.float32
+BF16 = mybir.dt.bfloat16
+I32 = mybir.dt.int32
+U32 = mybir.dt.uint32
+U8 = mybir.dt.uint8
+ALU = mybir.AluOpType
+ACTF = mybir.ActivationFunctionType
+AX = mybir.AxisListType
+
+P = 128
+B, T, D, H = 8, 16, 2048, 2048
+G = D // 512
+BANK = 512
+NB = H // BANK
+FLOPS = 2 * B * T * D * H * 3
+
+
+def tile_aftattention_w_kernel(
+    tc, x, Wq_words, Wq_scales, bq, Wk_words, Wk_scales, bk, Wv_words, Wv_scales, bv, wbias, out
+):
+    nc = tc.nc
+    with ExitStack() as ctx:
+        keep = ctx.enter_context(tc.tile_pool(name="keep", bufs=1))
+        psum = ctx.enter_context(tc.psum_pool(name="psum", bufs=1))
+        ctx.enter_context(tc.manual_schedule())
+
+        def bank(n, name):
+            return psum.tile([P, BANK], F32, name=name, tag="bank%d" % n)
+
+        planes = keep.tile([P, 3, H], U8, name="planes", align_bytes=64)
+        KI, VI, QI = 0, 1, 2
+        wk = [keep.tile([P, G, 4096], U8, name="wk%d" % r, align_bytes=64) for r in range(2)]
+        wv = [keep.tile([P, G, 4096], U8, name="wv%d" % r, align_bytes=64) for r in range(2)]
+        wq01 = keep.tile([P, G, 4096], U8, name="wq01", align_bytes=64)
+        wq2 = keep.tile([P, G, 2048], U8, name="wq2", align_bytes=64)
+        wq3 = keep.tile([P, G, 2048], U8, name="wq3", align_bytes=64)
+        x_sb = keep.tile([P, D], BF16, name="x_sb", align_bytes=64)
+        grouped = keep.tile([P, D // 2], F32, name="grouped", align_bytes=64)
+        xc = keep.tile([P, G * P], U32, name="xc", align_bytes=64)
+        xs = keep.tile([P, G * P], U8, name="xs", align_bytes=64)
+        ident = keep.tile([P, P], F32, name="ident")
+        ident_bf = keep.tile([P, P], BF16, name="ident_bf")
+        brow = keep.tile([P, P], BF16, name="brow")
+        bcol = keep.tile([P, 32], F32, name="bcol")
+        bqb = keep.tile([P, H], F32, name="bqb")
+        warm = keep.tile([P, 1], F32, name="warm")
+        warm_e = keep.tile([P, 1], F32, name="warm_e")
+        warm_s = keep.tile([P, 1], F32, name="warm_s")
+
+        for w in range(3):
+            nc.vector.memset(planes[:, w, :].bitcast(I32), 0)
+        nc.vector.memset(brow[:], 0.0)
+        nc.vector.memset(warm[:], 0.0)
+        make_identity(nc, ident[:])
+        make_identity(nc, ident_bf[:])
+
+        scales = ((KI, Wk_scales), (VI, Wv_scales), (QI, Wq_scales))
+
+        def load_scales(quadrants):
+            for w, sc in scales:
+                for q in quadrants:
+                    nc.sync.dma_start(
+                        out=planes[32 * q : 32 * q + 16, w, :].bitcast(I32),
+                        in_=sc[:, 4 * q : 4 * q + 4, :].bitcast(I32),
+                    )
+
+        def load_words(dst, src, g0, g1, c0, c1):
+            view = src.rearrange("g p n t -> p g (n t)").bitcast(I32)
+            nc.sync.dma_start(out=dst[:, g0:g1, :].bitcast(I32), in_=view[:, g0:g1, c0:c1])
+
+        nc.sync.dma_start(out=x_sb[:], in_=x.rearrange("b t d -> t b d"))
+        load_scales((2, 3))
+        load_scales((0, 1))
+        load_words(wk[0], Wk_words, 0, G, 0, 1024)
+        nc.sync.dma_start(out=brow[0:16, :], in_=bq.rearrange("(j c) -> j c", c=P))
+        nc.sync.dma_start(out=brow[16:32, :], in_=bv.rearrange("(j c) -> j c", c=P))
+        load_words(wv[0], Wv_words, 0, G, 0, 1024)
+        load_words(wk[1], Wk_words, 0, G, 1024, 2048)
+        load_words(wv[1], Wv_words, 0, G, 1024, 2048)
+        load_words(wq01, Wq_words, 0, G, 0, 1024)
+        load_words(wq2, Wq_words, 0, G, 1024, 1536)
+        load_words(wq3, Wq_words, 0, G - 1, 1536, 2048)
+        load_words(wq3, Wq_words, G - 1, G, 1536, 2048)
+
+        nc.scalar.activation(out=warm_e[:], in_=warm[:], func=ACTF.Exp)
+
+        x_words = x_sb[:].bitcast(F32)
+        xt = [bank(0, "xt0"), bank(1, "xt1")]
+        for g in range(G):
+            for u in range(2):
+                s = 2 * (g % 2) + u
+                nc.tensor.transpose(
+                    xt[g // 2][:, P * s : P * (s + 1)],
+                    x_words[:, 256 * g + u : 256 * (g + 1) : 2],
+                    ident[:],
+                )
+        for h, copy in ((0, nc.vector.tensor_copy), (1, nc.scalar.copy)):
+            copy(
+                out=grouped[:, 512 * h : 512 * (h + 1)].rearrange("p (g r u) -> p g r u", g=2, u=2),
+                in_=xt[h][:].rearrange("p (g u r) -> p g r u", g=2, u=2),
+            )
+        for h in range(2):
+            nc.vector.quantize_mx(
+                out=xc[:, 256 * h : 256 * (h + 1)].bitcast(FP8X4),
+                scales=xs[:, 256 * h : 256 * (h + 1)],
+                in_=grouped[:, 512 * h : 512 * (h + 1)].bitcast(BF16),
+            )
+
+        def project_t(ps, wt, wi, i):
+            for jj in range(4):
+                j = 4 * i + jj
+                jl = j % 8
+                for g in range(G):
+                    nc.tensor.matmul_mx(
+                        out=ps[:, P * jj : P * (jj + 1)],
+                        lhsT=wt[:, g, 512 * jl : 512 * (jl + 1)].bitcast(FP8X4),
+                        lhsT_scale=planes[4 * g : P, wi, P * j : P * (j + 1)],
+                        rhs=xc[:, P * g : P * (g + 1)].bitcast(FP8X4),
+                        rhs_scale=xs[:, P * g : P * (g + 1)],
+                        start=(g == 0),
+                        stop=(g == G - 1),
+                    )
+
+        def project_q(ps, wt, c0, i):
+            for g in range(G):
+                nc.tensor.matmul_mx(
+                    out=ps[:],
+                    lhsT=xc[:, P * g : P * (g + 1)].bitcast(FP8X4),
+                    lhsT_scale=xs[:, P * g : P * (g + 1)],
+                    rhs=wt[:, g, c0 : c0 + 4 * BANK].bitcast(FP8X4),
+                    rhs_scale=planes[4 * g : P, QI, BANK * i : BANK * (i + 1)],
+                    start=(g == 0),
+                    stop=(g == G - 1),
+                )
+
+        def by_b(ap):
+            return ap.rearrange("p (a b) -> p a b", b=B)
+
+        numer = [keep.tile([P, BANK], F32, name="numer%d" % i) for i in range(NB)]
+        nv = [keep.tile([P, BANK], F32, name="nv%d" % i) for i in range(NB)]
+        wtb = [keep.tile([P, BANK], F32, name="wtb%d" % i) for i in range(NB)]
+        z = [keep.tile([P, BANK], F32, name="z%d" % i) for i in range(NB)]
+        o = [keep.tile([P, BANK], F32, name="o%d" % i) for i in range(NB)]
+        mx = [keep.tile([P, 128], F32, name="mx%d" % r) for r in range(2)]
+        den = [keep.tile([P, 128], F32, name="den%d" % r) for r in range(2)]
+        rden = [keep.tile([P, 128], F32, name="rden%d" % r) for r in range(2)]
+        num = [keep.tile([P, 128], F32, name="num%d" % r) for r in range(2)]
+        w1 = [keep.tile([P, 128], F32, name="w1_%d" % r) for r in range(2)]
+        w2 = [keep.tile([P, 128], F32, name="w2_%d" % r) for r in range(2)]
+        wbp = [None] * NB
+
+        def k_stage(r, kbanks):
+            kp = []
+            for a in range(2):
+                i = 2 * r + a
+                kp.append(bank(kbanks[a], "kp%d" % i))
+                project_t(kp[a], wk[r], KI, i)
+            for a in range(2):
+                nc.vector.tensor_reduce(
+                    out=mx[r][:, 64 * a : 64 * (a + 1)], in_=by_b(kp[a][:]), axis=AX.X, op=ALU.max
+                )
+            for a in range(2):
+                i = 2 * r + a
+                nc.vector.tensor_tensor(
+                    out=by_b(numer[i][:]),
+                    in0=by_b(kp[a][:]),
+                    in1=mx[r][:, 64 * a : 64 * (a + 1)].unsqueeze(2).to_broadcast([P, 64, B]),
+                    op=ALU.subtract,
+                )
+                nc.scalar.activation(out=numer[i][:], in_=numer[i][:], func=ACTF.Exp)
+            for a in range(2):
+                i = 2 * r + a
+                nc.vector.tensor_reduce(
+                    out=den[r][:, 64 * a : 64 * (a + 1)], in_=by_b(numer[i][:]), axis=AX.X, op=ALU.add
+                )
+            nc.vector.reciprocal(out=rden[r][:], in_=den[r][:])
+
+        def v_passes(r, vbanks):
+            vp = []
+            for a in range(2):
+                i = 2 * r + a
+                vp.append(bank(vbanks[a], "vp%d" % i))
+                project_t(vp[a], wv[r], VI, i)
+            return vp
+
+        def v_epilogue(r, vp):
+            for a in range(2):
+                i = 2 * r + a
+                nc.vector.tensor_tensor(out=nv[i][:], in0=vp[a][:], in1=numer[i][:], op=ALU.mult)
+            for a in range(2):
+                i = 2 * r + a
+                nc.vector.tensor_reduce(
+                    out=num[r][:, 64 * a : 64 * (a + 1)], in_=by_b(nv[i][:]), axis=AX.X, op=ALU.add
+                )
+            nc.vector.tensor_tensor(out=w1[r][:], in0=num[r][:], in1=rden[r][:], op=ALU.mult)
+            nc.vector.tensor_tensor(
+                out=w2[r][:].rearrange("p (j t) -> p j t", t=T),
+                in0=w1[r][:].rearrange("p (j t) -> p j t", t=T),
+                in1=bcol[:, 16 + 8 * r : 16 + 8 * (r + 1)].unsqueeze(2).to_broadcast([P, 8, T]),
+                op=ALU.add,
+            )
+            for a in range(2):
+                i = 2 * r + a
+                nc.scalar.copy(
+                    out=by_b(wtb[i][:]),
+                    in_=w2[r][:, 64 * a : 64 * (a + 1)].unsqueeze(2).to_broadcast([P, 64, B]),
+                )
+
+        def w_transposes(r, banks):
+            for a in range(2):
+                i = 2 * r + a
+                wbp[i] = bank(banks[a], "wbp%d" % i)
+                for jj in range(4):
+                    nc.tensor.transpose(
+                        wbp[i][:, P * jj : P * (jj + 1)], wtb[i][:, P * jj : P * (jj + 1)], ident[:]
+                    )
+
+        out_v = out.rearrange("b t h -> t b h")
+
+        def q_add(i, qp, c0=0, c1=BANK):
+            nc.vector.tensor_tensor(
+                out=z[i][:, c0:c1],
+                in0=qp[:, c0:c1],
+                in1=bqb[:, BANK * i + c0 : BANK * i + c1],
+                op=ALU.add,
+            )
+            nc.scalar.activation(out=z[i][:, c0:c1], in_=z[i][:, c0:c1], func=ACTF.Sigmoid)
+
+        def q_mul(i, c0=0, c1=BANK):
+            nc.vector.tensor_tensor(
+                out=o[i][:, c0:c1], in0=wbp[i][:, c0:c1], in1=z[i][:, c0:c1], op=ALU.mult
+            )
+            nc.sync.dma_start(out=out_v[:, :, BANK * i + c0 : BANK * i + c1], in_=o[i][:, c0:c1])
+
+        k_stage(0, (0, 1))
+
+        bt = psum.tile([P, P], BF16, name="bt", tag="bank4")
+        nc.tensor.transpose(bt[:], brow[:], ident_bf[:])
+        nc.scalar.copy(out=bcol[:], in_=bt[:, 0:32])
+
+        vp = v_passes(0, (2, 3))
+
+        for i, n in enumerate((6, 7, 0, 1)):
+            bqp = bank(n, "bqp%d" % i)
+            for jj in range(4):
+                j = 4 * i + jj
+                nc.tensor.transpose(
+                    bqp[:, P * jj : P * (jj + 1)], bcol[:, j : j + 1].to_broadcast([P, P]), ident[:]
+                )
+            nc.scalar.copy(out=bqb[:, BANK * i : BANK * (i + 1)], in_=bqp[:])
+
+        v_epilogue(0, vp)
+        k_stage(1, (4, 5))
+        nc.scalar.activation(out=warm_s[:], in_=warm[:], func=ACTF.Sigmoid)
+        w_transposes(0, (0, 1))
+        vp = v_passes(1, (6, 7))
+        v_epilogue(1, vp)
+
+        qp0 = bank(2, "qp0")
+        project_q(qp0, wq01, 0, 0)
+        qp1 = bank(3, "qp1")
+        project_q(qp1, wq01, 4 * BANK, 1)
+        w_transposes(1, (4, 5))
+        q_add(0, qp0)
+        q_add(1, qp1)
+        q_mul(0)
+        q_mul(1)
+        qp2 = bank(6, "qp2")
+        project_q(qp2, wq2, 0, 2)
+        q_add(2, qp2)
+        q_mul(2)
+        qp3 = bank(7, "qp3")
+        project_q(qp3, wq3, 0, 3)
+        q_add(3, qp3, 0, 256)
+        q_add(3, qp3, 256, 512)
+        q_mul(3, 0, 256)
+        q_mul(3, 256, 512)

@@ -70,9 +70,11 @@ def tile_aftattention_w_kernel(
                         in_=sc[:, 4 * q : 4 * q + 4, :].bitcast(I32),
                     )
 
-        def load_words(dst, src, g0, g1, c0, c1):
+        def load_words(dst, src, g0, g1, c0, c1, d0=0):
             view = src.rearrange("g p n t -> p g (n t)").bitcast(I32)
-            nc.sync.dma_start(out=dst[:, g0:g1, :].bitcast(I32), in_=view[:, g0:g1, c0:c1])
+            nc.sync.dma_start(
+                out=dst[:, g0:g1, d0 : d0 + 4 * (c1 - c0)].bitcast(I32), in_=view[:, g0:g1, c0:c1]
+            )
 
         nc.sync.dma_start(out=x_sb[:], in_=x.rearrange("b t d -> t b d"))
         load_scales((2, 3))
@@ -84,9 +86,11 @@ def tile_aftattention_w_kernel(
         load_words(wk[1], Wk_words, 0, G, 1024, 2048)
         load_words(wv[1], Wv_words, 0, G, 1024, 2048)
         load_words(wq01, Wq_words, 0, G, 0, 1024)
-        load_words(wq2, Wq_words, 0, G, 1024, 1536)
+        load_words(wq2, Wq_words, 0, G - 1, 1024, 1536)
+        load_words(wq2, Wq_words, G - 1, G, 1024, 1536)
         load_words(wq3, Wq_words, 0, G - 1, 1536, 2048)
-        load_words(wq3, Wq_words, G - 1, G, 1536, 2048)
+        load_words(wq3, Wq_words, G - 1, G, 1536, 1792)
+        load_words(wq3, Wq_words, G - 1, G, 1792, 2048, 1024)
 
         nc.scalar.activation(out=warm_e[:], in_=warm[:], func=ACTF.Exp)
 
@@ -127,14 +131,14 @@ def tile_aftattention_w_kernel(
                         stop=(g == G - 1),
                     )
 
-        def project_q(ps, wt, c0, i):
-            for g in range(G):
+        def project_q(ps, wt, d0, h0, n, gs):
+            for g in gs:
                 nc.tensor.matmul_mx(
-                    out=ps[:],
+                    out=ps,
                     lhsT=xc[:, P * g : P * (g + 1)].bitcast(FP8X4),
                     lhsT_scale=xs[:, P * g : P * (g + 1)],
-                    rhs=wt[:, g, c0 : c0 + 4 * BANK].bitcast(FP8X4),
-                    rhs_scale=planes[4 * g : P, QI, BANK * i : BANK * (i + 1)],
+                    rhs=wt[:, g, d0 : d0 + 4 * n].bitcast(FP8X4),
+                    rhs_scale=planes[4 * g : P, QI, h0 : h0 + n],
                     start=(g == 0),
                     stop=(g == G - 1),
                 )
@@ -226,7 +230,7 @@ def tile_aftattention_w_kernel(
         def q_add(i, qp, c0=0, c1=BANK):
             nc.vector.tensor_tensor(
                 out=z[i][:, c0:c1],
-                in0=qp[:, c0:c1],
+                in0=qp,
                 in1=bqb[:, BANK * i + c0 : BANK * i + c1],
                 op=ALU.add,
             )
@@ -263,21 +267,24 @@ def tile_aftattention_w_kernel(
         v_epilogue(1, vp)
 
         qp0 = bank(2, "qp0")
-        project_q(qp0, wq01, 0, 0)
+        project_q(qp0[:], wq01, 0, 0, BANK, range(G))
         qp1 = bank(3, "qp1")
-        project_q(qp1, wq01, 4 * BANK, 1)
+        project_q(qp1[:], wq01, 4 * BANK, BANK, BANK, range(G))
+        q_add(0, qp0[:])
+        q_add(1, qp1[:])
+        qp2 = bank(6, "qp2")
+        project_q(qp2[:], wq2, 0, 2 * BANK, BANK, range(G))
         w_transposes(1, (4, 5))
-        q_add(0, qp0)
-        q_add(1, qp1)
         q_mul(0)
         q_mul(1)
-        qp2 = bank(6, "qp2")
-        project_q(qp2, wq2, 0, 2)
-        q_add(2, qp2)
+        q_add(2, qp2[:])
+        half = BANK // 2
+        qp3 = [bank(7, "qp3a"), bank(2, "qp3b")]
+        for gs in (range(G - 1), range(G - 1, G)):
+            for a in range(2):
+                project_q(qp3[a][:, 0:half], wq3, 4 * half * a, 3 * BANK + half * a, half, gs)
+        for a in range(2):
+            q_add(3, qp3[a][:, 0:half], half * a, half * (a + 1))
         q_mul(2)
-        qp3 = bank(7, "qp3")
-        project_q(qp3, wq3, 0, 3)
-        q_add(3, qp3, 0, 256)
-        q_add(3, qp3, 256, 512)
-        q_mul(3, 0, 256)
-        q_mul(3, 256, 512)
+        for a in range(2):
+            q_mul(3, half * a, half * (a + 1))

@@ -62,8 +62,8 @@ def tile_aftattention_w_kernel(
 
         scales = ((KI, Wk_scales), (VI, Wv_scales), (QI, Wq_scales))
 
-        def load_scales(quadrants):
-            for w, sc in scales:
+        def load_scales(quadrants, which):
+            for w, sc in which:
                 for q in quadrants:
                     nc.sync.dma_start(
                         out=planes[32 * q : 32 * q + 16, w, :].bitcast(I32),
@@ -77,9 +77,10 @@ def tile_aftattention_w_kernel(
             )
 
         nc.sync.dma_start(out=x_sb[:], in_=x.rearrange("b t d -> t b d"))
-        load_scales((2, 3))
-        load_scales((0, 1))
+        load_scales((2, 3), scales)
+        load_scales((0, 1), scales[0:1])
         load_words(wk[0], Wk_words, 0, G, 0, 1024)
+        load_scales((0, 1), scales[1:3])
         nc.sync.dma_start(out=brow[0:16, :], in_=bq.rearrange("(j c) -> j c", c=P))
         nc.sync.dma_start(out=brow[16:32, :], in_=bv.rearrange("(j c) -> j c", c=P))
         load_words(wv[0], Wv_words, 0, G, 0, 1024)

@@ -78,9 +78,8 @@ def tile_aftattention_w_kernel(
 
         nc.sync.dma_start(out=x_sb[:], in_=x.rearrange("b t d -> t b d"))
         load_scales((2, 3), scales)
-        load_scales((0, 1), scales[0:1])
         load_words(wk[0], Wk_words, 0, G, 0, 1024)
-        load_scales((0, 1), scales[1:3])
+        load_scales((0, 1), scales)
         nc.sync.dma_start(out=brow[0:16, :], in_=bq.rearrange("(j c) -> j c", c=P))
         nc.sync.dma_start(out=brow[16:32, :], in_=bv.rearrange("(j c) -> j c", c=P))
         load_words(wv[0], Wv_words, 0, G, 0, 1024)

@@ -78,8 +78,9 @@ def tile_aftattention_w_kernel(
 
         nc.sync.dma_start(out=x_sb[:], in_=x.rearrange("b t d -> t b d"))
         load_scales((2, 3), scales)
+        load_scales((0, 1), scales[0:1])
         load_words(wk[0], Wk_words, 0, G, 0, 1024)
-        load_scales((0, 1), scales)
+        load_scales((0, 1), scales[1:3])
         nc.sync.dma_start(out=brow[0:16, :], in_=bq.rearrange("(j c) -> j c", c=P))
         nc.sync.dma_start(out=brow[16:32, :], in_=bv.rearrange("(j c) -> j c", c=P))
         load_words(wv[0], Wv_words, 0, G, 0, 1024)
@@ -151,7 +152,6 @@ def tile_aftattention_w_kernel(
         wtb = [keep.tile([P, BANK], F32, name="wtb%d" % i) for i in range(NB)]
         z = [keep.tile([P, BANK], F32, name="z%d" % i) for i in range(NB)]
         o = [keep.tile([P, BANK], F32, name="o%d" % i) for i in range(NB)]
-        mx = [keep.tile([P, 128], F32, name="mx%d" % r) for r in range(2)]
         den = [keep.tile([P, 128], F32, name="den%d" % r) for r in range(2)]
         rden = [keep.tile([P, 128], F32, name="rden%d" % r) for r in range(2)]
         num = [keep.tile([P, 128], F32, name="num%d" % r) for r in range(2)]
@@ -166,18 +166,8 @@ def tile_aftattention_w_kernel(
                 kp.append(bank(kbanks[a], "kp%d" % i))
                 project_t(kp[a], wk[r], KI, i)
             for a in range(2):
-                nc.vector.tensor_reduce(
-                    out=mx[r][:, 64 * a : 64 * (a + 1)], in_=by_b(kp[a][:]), axis=AX.X, op=ALU.max
-                )
-            for a in range(2):
                 i = 2 * r + a
-                nc.vector.tensor_tensor(
-                    out=by_b(numer[i][:]),
-                    in0=by_b(kp[a][:]),
-                    in1=mx[r][:, 64 * a : 64 * (a + 1)].unsqueeze(2).to_broadcast([P, 64, B]),
-                    op=ALU.subtract,
-                )
-                nc.scalar.activation(out=numer[i][:], in_=numer[i][:], func=ACTF.Exp)
+                nc.scalar.activation(out=numer[i][:], in_=kp[a][:], func=ACTF.Exp)
             for a in range(2):
                 i = 2 * r + a
                 nc.vector.tensor_reduce(

from contextlib import ExitStack

import concourse.mybir as mybir
from concourse.masks import make_identity

FP8X4 = mybir.dt.float8_e4m3fn_x4
F32 = mybir.dt.float32
BF16 = mybir.dt.bfloat16
I32 = mybir.dt.int32
U32 = mybir.dt.uint32
U8 = mybir.dt.uint8
ALU = mybir.AluOpType
ACTF = mybir.ActivationFunctionType
AX = mybir.AxisListType

P = 128
B, T, D, H = 8, 16, 2048, 2048
G = D // 512
BANK = 512
NB = H // BANK
FLOPS = 2 * B * T * D * H * 3


def tile_aftattention_w_kernel(
    tc, x, Wq_words, Wq_scales, bq, Wk_words, Wk_scales, bk, Wv_words, Wv_scales, bv, wbias, out
):
    nc = tc.nc
    with ExitStack() as ctx:
        keep = ctx.enter_context(tc.tile_pool(name="keep", bufs=1))
        psum = ctx.enter_context(tc.psum_pool(name="psum", bufs=1))
        ctx.enter_context(tc.manual_schedule())

        def bank(n, name):
            return psum.tile([P, BANK], F32, name=name, tag="bank%d" % n)

        planes = keep.tile([P, 3, H], U8, name="planes", align_bytes=64)
        KI, VI, QI = 0, 1, 2
        wk = [keep.tile([P, G, 4096], U8, name="wk%d" % r, align_bytes=64) for r in range(2)]
        wv = [keep.tile([P, G, 4096], U8, name="wv%d" % r, align_bytes=64) for r in range(2)]
        wq01 = keep.tile([P, G, 4096], U8, name="wq01", align_bytes=64)
        wq2 = keep.tile([P, G, 2048], U8, name="wq2", align_bytes=64)
        wq3 = keep.tile([P, G, 2048], U8, name="wq3", align_bytes=64)
        x_sb = keep.tile([P, D], BF16, name="x_sb", align_bytes=64)
        grouped = keep.tile([P, D // 2], F32, name="grouped", align_bytes=64)
        xc = keep.tile([P, G * P], U32, name="xc", align_bytes=64)
        xs = keep.tile([P, G * P], U8, name="xs", align_bytes=64)
        ident = keep.tile([P, P], F32, name="ident")
        ident_bf = keep.tile([P, P], BF16, name="ident_bf")
        brow = keep.tile([P, P], BF16, name="brow")
        bcol = keep.tile([P, 32], F32, name="bcol")
        bqb = keep.tile([P, H], F32, name="bqb")
        warm = keep.tile([P, 1], F32, name="warm")
        warm_e = keep.tile([P, 1], F32, name="warm_e")
        warm_s = keep.tile([P, 1], F32, name="warm_s")

        for w in range(3):
            nc.vector.memset(planes[:, w, :].bitcast(I32), 0)
        nc.vector.memset(brow[:], 0.0)
        nc.vector.memset(warm[:], 0.0)
        make_identity(nc, ident[:])
        make_identity(nc, ident_bf[:])

        scales = ((KI, Wk_scales), (VI, Wv_scales), (QI, Wq_scales))

        def load_scales(quadrants, which):
            for w, sc in which:
                for q in quadrants:
                    nc.sync.dma_start(
                        out=planes[32 * q : 32 * q + 16, w, :].bitcast(I32),
                        in_=sc[:, 4 * q : 4 * q + 4, :].bitcast(I32),
                    )

        def load_words(dst, src, g0, g1, c0, c1, d0=0):
            view = src.rearrange("g p n t -> p g (n t)").bitcast(I32)
            nc.sync.dma_start(
                out=dst[:, g0:g1, d0 : d0 + 4 * (c1 - c0)].bitcast(I32), in_=view[:, g0:g1, c0:c1]
            )

        nc.sync.dma_start(out=x_sb[:], in_=x.rearrange("b t d -> t b d"))
        load_scales((2, 3), scales)
        load_scales((0, 1), scales[0:1])
        load_words(wk[0], Wk_words, 0, G, 0, 1024)
        load_scales((0, 1), scales[1:3])
        nc.sync.dma_start(out=brow[0:16, :], in_=bq.rearrange("(j c) -> j c", c=P))
        nc.sync.dma_start(out=brow[16:32, :], in_=bv.rearrange("(j c) -> j c", c=P))
        load_words(wv[0], Wv_words, 0, G, 0, 1024)
        load_words(wk[1], Wk_words, 0, G, 1024, 2048)
        load_words(wv[1], Wv_words, 0, G, 1024, 2048)
        load_words(wq01, Wq_words, 0, G, 0, 1024)
        load_words(wq2, Wq_words, 0, G - 1, 1024, 1536)
        load_words(wq2, Wq_words, G - 1, G, 1024, 1536)
        load_words(wq3, Wq_words, 0, G - 1, 1536, 2048)
        load_words(wq3, Wq_words, G - 1, G, 1536, 1792)
        load_words(wq3, Wq_words, G - 1, G, 1792, 2048, 1024)

        nc.scalar.activation(out=warm_e[:], in_=warm[:], func=ACTF.Exp)

        x_words = x_sb[:].bitcast(F32)
        xt = [bank(0, "xt0"), bank(1, "xt1")]
        for g in range(G):
            for u in range(2):
                s = 2 * (g % 2) + u
                nc.tensor.transpose(
                    xt[g // 2][:, P * s : P * (s + 1)],
                    x_words[:, 256 * g + u : 256 * (g + 1) : 2],
                    ident[:],
                )
        for h, copy in ((0, nc.vector.tensor_copy), (1, nc.scalar.copy)):
            copy(
                out=grouped[:, 512 * h : 512 * (h + 1)].rearrange("p (g r u) -> p g r u", g=2, u=2),
                in_=xt[h][:].rearrange("p (g u r) -> p g r u", g=2, u=2),
            )
        for h in range(2):
            nc.vector.quantize_mx(
                out=xc[:, 256 * h : 256 * (h + 1)].bitcast(FP8X4),
                scales=xs[:, 256 * h : 256 * (h + 1)],
                in_=grouped[:, 512 * h : 512 * (h + 1)].bitcast(BF16),
            )

        def project_t(ps, wt, wi, i):
            for jj in range(4):
                j = 4 * i + jj
                jl = j % 8
                for g in range(G):
                    nc.tensor.matmul_mx(
                        out=ps[:, P * jj : P * (jj + 1)],
                        lhsT=wt[:, g, 512 * jl : 512 * (jl + 1)].bitcast(FP8X4),
                        lhsT_scale=planes[4 * g : P, wi, P * j : P * (j + 1)],
                        rhs=xc[:, P * g : P * (g + 1)].bitcast(FP8X4),
                        rhs_scale=xs[:, P * g : P * (g + 1)],
                        start=(g == 0),
                        stop=(g == G - 1),
                    )

        def project_q(ps, wt, d0, h0, n, gs):
            for g in gs:
                nc.tensor.matmul_mx(
                    out=ps,
                    lhsT=xc[:, P * g : P * (g + 1)].bitcast(FP8X4),
                    lhsT_scale=xs[:, P * g : P * (g + 1)],
                    rhs=wt[:, g, d0 : d0 + 4 * n].bitcast(FP8X4),
                    rhs_scale=planes[4 * g : P, QI, h0 : h0 + n],
                    start=(g == 0),
                    stop=(g == G - 1),
                )

        def by_b(ap):
            return ap.rearrange("p (a b) -> p a b", b=B)

        numer = [keep.tile([P, BANK], F32, name="numer%d" % i) for i in range(NB)]
        nv = [keep.tile([P, BANK], F32, name="nv%d" % i) for i in range(NB)]
        wtb = [keep.tile([P, BANK], F32, name="wtb%d" % i) for i in range(NB)]
        z = [keep.tile([P, BANK], F32, name="z%d" % i) for i in range(NB)]
        o = [keep.tile([P, BANK], F32, name="o%d" % i) for i in range(NB)]
        den = [keep.tile([P, 128], F32, name="den%d" % r) for r in range(2)]
        rden = [keep.tile([P, 128], F32, name="rden%d" % r) for r in range(2)]
        num = [keep.tile([P, 128], F32, name="num%d" % r) for r in range(2)]
        w1 = [keep.tile([P, 128], F32, name="w1_%d" % r) for r in range(2)]
        w2 = [keep.tile([P, 128], F32, name="w2_%d" % r) for r in range(2)]
        wbp = [None] * NB

        def k_stage(r, kbanks):
            kp = []
            for a in range(2):
                i = 2 * r + a
                kp.append(bank(kbanks[a], "kp%d" % i))
                project_t(kp[a], wk[r], KI, i)
            for a in range(2):
                i = 2 * r + a
                nc.scalar.activation(out=numer[i][:], in_=kp[a][:], func=ACTF.Exp)
            for a in range(2):
                i = 2 * r + a
                nc.vector.tensor_reduce(
                    out=den[r][:, 64 * a : 64 * (a + 1)], in_=by_b(numer[i][:]), axis=AX.X, op=ALU.add
                )
            nc.vector.reciprocal(out=rden[r][:], in_=den[r][:])

        def v_passes(r, vbanks):
            vp = []
            for a in range(2):
                i = 2 * r + a
                vp.append(bank(vbanks[a], "vp%d" % i))
                project_t(vp[a], wv[r], VI, i)
            return vp

        def v_epilogue(r, vp):
            for a in range(2):
                i = 2 * r + a
                nc.vector.tensor_tensor(out=nv[i][:], in0=vp[a][:], in1=numer[i][:], op=ALU.mult)
            for a in range(2):
                i = 2 * r + a
                nc.vector.tensor_reduce(
                    out=num[r][:, 64 * a : 64 * (a + 1)], in_=by_b(nv[i][:]), axis=AX.X, op=ALU.add
                )
            nc.vector.tensor_tensor(out=w1[r][:], in0=num[r][:], in1=rden[r][:], op=ALU.mult)
            nc.vector.tensor_tensor(
                out=w2[r][:].rearrange("p (j t) -> p j t", t=T),
                in0=w1[r][:].rearrange("p (j t) -> p j t", t=T),
                in1=bcol[:, 16 + 8 * r : 16 + 8 * (r + 1)].unsqueeze(2).to_broadcast([P, 8, T]),
                op=ALU.add,
            )
            for a in range(2):
                i = 2 * r + a
                nc.scalar.copy(
                    out=by_b(wtb[i][:]),
                    in_=w2[r][:, 64 * a : 64 * (a + 1)].unsqueeze(2).to_broadcast([P, 64, B]),
                )

        def w_transposes(r, banks):
            for a in range(2):
                i = 2 * r + a
                wbp[i] = bank(banks[a], "wbp%d" % i)
                for jj in range(4):
                    nc.tensor.transpose(
                        wbp[i][:, P * jj : P * (jj + 1)], wtb[i][:, P * jj : P * (jj + 1)], ident[:]
                    )

        out_v = out.rearrange("b t h -> t b h")

        def q_add(i, qp, c0=0, c1=BANK):
            nc.vector.tensor_tensor(
                out=z[i][:, c0:c1],
                in0=qp,
                in1=bqb[:, BANK * i + c0 : BANK * i + c1],
                op=ALU.add,
            )
            nc.scalar.activation(out=z[i][:, c0:c1], in_=z[i][:, c0:c1], func=ACTF.Sigmoid)

        def q_mul(i, c0=0, c1=BANK):
            nc.vector.tensor_tensor(
                out=o[i][:, c0:c1], in0=wbp[i][:, c0:c1], in1=z[i][:, c0:c1], op=ALU.mult
            )
            nc.sync.dma_start(out=out_v[:, :, BANK * i + c0 : BANK * i + c1], in_=o[i][:, c0:c1])

        k_stage(0, (0, 1))

        bt = psum.tile([P, P], BF16, name="bt", tag="bank4")
        nc.tensor.transpose(bt[:], brow[:], ident_bf[:])
        nc.scalar.copy(out=bcol[:], in_=bt[:, 0:32])

        vp = v_passes(0, (2, 3))

        for i, n in enumerate((6, 7, 0, 1)):
            bqp = bank(n, "bqp%d" % i)
            for jj in range(4):
                j = 4 * i + jj
                nc.tensor.transpose(
                    bqp[:, P * jj : P * (jj + 1)], bcol[:, j : j + 1].to_broadcast([P, P]), ident[:]
                )
            nc.scalar.copy(out=bqb[:, BANK * i : BANK * (i + 1)], in_=bqp[:])

        v_epilogue(0, vp)
        k_stage(1, (4, 5))
        nc.scalar.activation(out=warm_s[:], in_=warm[:], func=ACTF.Sigmoid)
        w_transposes(0, (0, 1))
        vp = v_passes(1, (6, 7))
        v_epilogue(1, vp)

        qp0 = bank(2, "qp0")
        project_q(qp0[:], wq01, 0, 0, BANK, range(G))
        qp1 = bank(3, "qp1")
        project_q(qp1[:], wq01, 4 * BANK, BANK, BANK, range(G))
        q_add(0, qp0[:])
        q_add(1, qp1[:])
        qp2 = bank(6, "qp2")
        project_q(qp2[:], wq2, 0, 2 * BANK, BANK, range(G))
        w_transposes(1, (4, 5))
        q_mul(0)
        q_mul(1)
        q_add(2, qp2[:])
        half = BANK // 2
        qp3 = [bank(7, "qp3a"), bank(2, "qp3b")]
        for gs in (range(G - 1), range(G - 1, G)):
            for a in range(2):
                project_q(qp3[a][:, 0:half], wq3, 4 * half * a, 3 * BANK + half * a, half, gs)
        for a in range(2):
            q_add(3, qp3[a][:, 0:half], half * a, half * (a + 1))
        q_mul(2)
        for a in range(2):
            q_mul(3, half * a, half * (a + 1))
